import numpy as np
import ml_dtypes


def mxq(x, axis, fmt="e4m3"):
    dtype, down = {"e4m3": (ml_dtypes.float8_e4m3fn, 7), "e5m2": (ml_dtypes.float8_e5m2, 14)}[fmt]
    v = np.moveaxis(np.asarray(x, np.float32).astype(ml_dtypes.bfloat16).astype(np.float64), axis, -1)
    blocks = v.reshape(v.shape[:-1] + (-1, 32))
    amax = np.abs(blocks).max(-1, keepdims=True)
    byte = np.maximum(np.where(amax > 0, np.frexp(amax)[1] - 1 + 127, 0) - down, 1)
    scale = np.exp2(byte - 127.0)
    codes = (blocks / scale).astype(np.float32).astype(dtype).astype(np.float64)
    return np.moveaxis((codes * scale).reshape(v.shape), -1, axis)


WIDE = False


def mx_kscale(k):
    if not WIDE:
        return np.ones(k)
    levels = np.array([10, -10, 5, -5, 0])
    a = np.random.permutation(np.resize(levels, k // 512 * 4)).reshape(k // 512, 4)
    idx = np.arange(k)
    return np.exp2(a[idx // 512, idx % 128 // 32])


BF16 = ml_dtypes.bfloat16


def bf(x):
    return np.asarray(x, np.float32).astype(BF16)


def f64(x):
    return np.asarray(x).astype(np.float64)


B, DIN, H0, H1, L, C, K = 1024, 1024, 2048, 1024, 512, 64, 64
BETA = 10.0


def logsumexp(a):
    m = a.max(-1, keepdims=True)
    return (m + np.log(np.exp(a - m).sum(-1, keepdims=True)))[..., 0]


def setup_inputs():
    s, t = mx_kscale(H1), mx_kscale(L)
    return {"h_enc": bf(np.maximum(np.random.standard_normal((B, H1)), 0.0) * s),
            "enc_w2": bf(np.random.standard_normal((H1, L)) * np.sqrt(2.0 / H1) / s[:, None] * t),
            "enc_b2": bf(np.random.standard_normal(L) * 0.1 * t),
            "clus_w": bf(np.random.standard_normal((C, K, L)) * 0.3 / np.sqrt(L) / t),
            "clus_b": bf(np.random.standard_normal((C, K)) * 0.1)}


def reference(h_enc, enc_w2, enc_b2, clus_w, clus_b):
    z = (mxq(f64(h_enc), 1, "e4m3") @ mxq(f64(enc_w2), 0, "e4m3")) + f64(enc_b2)
    wq = mxq(f64(clus_w), 2, "e4m3")
    scores = (mxq(z, 1, "e4m3") @ wq.reshape(C * K, L).T).reshape(B, C, K) + f64(clus_b)
    conf = -logsumexp(-BETA * scores)
    return z, conf

@@ -1,0 +1,247 @@
+import concourse.mybir as mybir
+from concourse.masks import make_identity
+
+F32 = mybir.dt.float32
+BF16 = mybir.dt.bfloat16
+U32 = mybir.dt.uint32
+U8 = mybir.dt.uint8
+FP8X4 = mybir.dt.float8_e4m3fn_x4
+ALU = mybir.AluOpType
+ACT = mybir.ActivationFunctionType
+AXIS = mybir.AxisListType
+
+P = 128
+PACK = 4
+BATCH, HIDDEN, LATENT, MODULES, HEADS = 1024, 1024, 512, 64, 64
+BETA = 10.0
+B_TILES = BATCH // P
+PASSES_1 = HIDDEN // (P * PACK)
+BANK = 512
+CHUNKS = MODULES * HEADS // BANK
+MODS = BANK // HEADS
+ROW_TILES = BANK // P
+GROUP = 4
+
+FLOPS = 2 * BATCH * HIDDEN * LATENT + 2 * BATCH * LATENT * MODULES * HEADS
+
+
+def tile_ace_pa_kernel(tc, h_enc, enc_w2, enc_b2, clus_w, clus_b, out_0, out_1):
+    nc = tc.nc
+    h_view = h_enc.rearrange("(p t) k -> p t k", t=B_TILES)
+    z_view = out_0.rearrange("(p t) d -> p t d", t=B_TILES)
+    conf_view = out_1.rearrange("(p t) c -> p (t c)", t=B_TILES)
+    cw_view = clus_w.rearrange("c k d -> (c k) d").rearrange("(r p) d -> p r d", p=P)
+
+    with tc.tile_pool(name="keep", bufs=1) as keep, tc.tile_pool(name="stage", bufs=2) as stage, tc.tile_pool(
+        name="work", bufs=3
+    ) as work, tc.psum_pool(name="ps_t", bufs=2) as ps_t, tc.psum_pool(name="ps_1", bufs=1) as ps_1, tc.psum_pool(
+        name="ps_s", bufs=4
+    ) as ps_s:
+        bias_rows = keep.tile([P, CHUNKS * BANK + LATENT], BF16)
+        nc.vector.memset(bias_rows[:].bitcast(F32), 0.0)
+        b2_words = keep.tile([P, P], F32)
+        nc.vector.memset(b2_words[:], 0.0)
+        nc.scalar.dma_start(out=bias_rows[0:1, 0 : CHUNKS * BANK], in_=clus_b.rearrange("c k -> (c k)").unsqueeze(0))
+        nc.scalar.dma_start(out=bias_rows[0:1, CHUNKS * BANK :], in_=enc_b2.unsqueeze(0))
+        nc.scalar.dma_start(out=b2_words[0:2, :], in_=enc_b2.bitcast(F32).rearrange("(u q) -> u q", u=2))
+
+        w2_raw = keep.tile([P, 2 * PASSES_1, 2 * LATENT], BF16)
+        nc.sync.dma_start(out=w2_raw[:], in_=enc_w2.rearrange("(w p e) d -> p w (e d)", w=2 * PASSES_1, e=2))
+        h_sb = keep.tile([P, B_TILES * HIDDEN], BF16)
+        for t in range(0, B_TILES, 2):
+            nc.sync.dma_start(
+                out=h_sb[:, t * HIDDEN : (t + 2) * HIDDEN].rearrange("p (t k) -> p t k", t=2), in_=h_view[:, t : t + 2, :]
+            )
+        cw_sb = keep.tile([P, CHUNKS * ROW_TILES * LATENT], BF16)
+        for j in range(CHUNKS):
+            nc.sync.dma_start(
+                out=cw_sb[:, j * ROW_TILES * LATENT : (j + 1) * ROW_TILES * LATENT].rearrange(
+                    "p (r d) -> p r d", r=ROW_TILES
+                ),
+                in_=cw_view[:, j * ROW_TILES : (j + 1) * ROW_TILES, :],
+            )
+        h_words = h_sb[:].bitcast(F32)
+        cw_words = cw_sb[:].bitcast(F32)
+
+        ident = keep.tile([P, P], F32)
+        make_identity(nc, ident[:])
+        ones = keep.tile([P, P], BF16)
+        nc.vector.memset(ones[:], 1.0)
+        warm_in = keep.tile([P, 1], F32)
+        nc.vector.memset(warm_in[:], 0.0)
+        warm_out = keep.tile([P, 1], F32)
+        nc.scalar.activation(out=warm_out[:], in_=warm_in[:], func=ACT.Exp)
+
+        bias10 = keep.tile([P, CHUNKS, BANK], F32)
+        for j in range(CHUNKS):
+            spread = ps_s.tile([P, BANK], F32, tag="bank")
+            nc.tensor.matmul(spread[:], lhsT=ones[:], rhs=bias_rows[:, j * BANK : (j + 1) * BANK], start=True, stop=True)
+            nc.scalar.mul(out=bias10[:, j, :], in_=spread[:], mul=BETA)
+        b2_free = keep.tile([P, LATENT], F32)
+        spread = ps_s.tile([P, BANK], F32, tag="bank")
+        nc.tensor.matmul(spread[:], lhsT=ones[:], rhs=bias_rows[:, CHUNKS * BANK :], start=True, stop=True)
+        nc.scalar.copy(out=b2_free[:], in_=spread[:])
+        flipped = ps_t.tile([P, PACK, P], F32, tag="flip")
+        nc.tensor.transpose(flipped[:, 0, :], b2_words[:], ident[:])
+        b2_pairs = keep.tile([P, 2], F32)
+        nc.vector.tensor_copy(out=b2_pairs[:], in_=flipped[:, 0, 0:2])
+        b2_part = keep.tile([P, PACK], F32)
+        nc.vector.tensor_copy(out=b2_part[:], in_=b2_pairs[:].bitcast(BF16))
+
+        w2_grouped = keep.tile([P, PASSES_1, LATENT, PACK], BF16, align_bytes=64)
+        w2_codes = keep.tile([P, PASSES_1, LATENT], U32, align_bytes=64)
+        w2_scales = keep.tile([P, PASSES_1, LATENT], U8, align_bytes=64)
+        for g in range(PASSES_1):
+            for u in range(2):
+                nc.vector.tensor_copy(
+                    out=w2_grouped[:, g, 256 * u : 256 * (u + 1), :].rearrange("p (e q) j -> p e q j", e=2),
+                    in_=w2_raw[:, 2 * g : 2 * g + 2, :]
+                    .rearrange("p w (e d) -> p (w e) d", e=2)[:, :, 256 * u : 256 * (u + 1)]
+                    .rearrange("p j (q e) -> p e q j", e=2),
+                )
+        for g in range(PASSES_1):
+            nc.vector.quantize_mx(
+                out=w2_codes[:, g, :].bitcast(FP8X4),
+                scales=w2_scales[:, g, :],
+                in_=w2_grouped[:, g, :, :].rearrange("p d j -> p (d j)"),
+            )
+
+        w_codes = keep.tile([P, CHUNKS, BANK], U32, align_bytes=64)
+        w_scales = keep.tile([P, CHUNKS, BANK], U8, align_bytes=64)
+
+        def prepare_chunk(j):
+            w_grouped = stage.tile([P, BANK * PACK], BF16, align_bytes=64)
+            for half in range(2):
+                flip_w = ps_t.tile([P, PACK, P], F32, tag="flip")
+                for u in range(2):
+                    for rr in range(2):
+                        r = j * ROW_TILES + 2 * half + rr
+                        nc.tensor.transpose(
+                            flip_w[:, 2 * u + rr, :],
+                            cw_words[:, r * 256 + u * P : r * 256 + (u + 1) * P],
+                            ident[:],
+                        )
+                nc.scalar.copy(
+                    out=w_grouped[:, half * 1024 : (half + 1) * 1024].bitcast(F32).rearrange("p (n u) -> p n u", u=2),
+                    in_=flip_w[:].rearrange("p (u r) q -> p (r q) u", u=2),
+                )
+            nc.vector.quantize_mx(out=w_codes[:, j, :].bitcast(FP8X4), scales=w_scales[:, j, :], in_=w_grouped[:])
+
+        h_codes = keep.tile([P, B_TILES, PASSES_1 * P], U32, align_bytes=64)
+        h_scales = keep.tile([P, B_TILES, PASSES_1 * P], U8, align_bytes=64)
+        z_sb = keep.tile([P, B_TILES, LATENT], F32)
+        z_codes = keep.tile([P, B_TILES, P], U32, align_bytes=64)
+        z_scales = keep.tile([P, B_TILES, P], U8, align_bytes=64)
+
+        def quantise_h(t):
+            flip_h = ps_t.tile([P, PACK, P], F32, tag="flip")
+            for w in range(2 * PASSES_1):
+                nc.tensor.transpose(
+                    flip_h[:, w, :], h_words[:, t * 512 + w * P : t * 512 + (w + 1) * P], ident[:]
+                )
+            h_grouped = stage.tile([P, PASSES_1 * P * PACK], BF16, align_bytes=64)
+            nc.scalar.copy(
+                out=h_grouped[:].bitcast(F32).rearrange("p (g b u) -> p g b u", g=PASSES_1, u=2),
+                in_=flip_h[:].rearrange("p (g u) b -> p g b u", u=2),
+            )
+            nc.vector.quantize_mx(out=h_codes[:, t, :].bitcast(FP8X4), scales=h_scales[:, t, :], in_=h_grouped[:])
+
+        def first_product(t):
+            z_ps = ps_1.tile([P, LATENT], F32, tag="z")
+            for g in range(PASSES_1):
+                nc.tensor.matmul_mx(
+                    out=z_ps[:],
+                    lhsT=h_codes[:, t, g * P : (g + 1) * P].bitcast(FP8X4),
+                    lhsT_scale=h_scales[:, t, g * P : (g + 1) * P],
+                    rhs=w2_codes[:, g, :].bitcast(FP8X4),
+                    rhs_scale=w2_scales[:, g, :],
+                    start=(g == 0),
+                    stop=(g == PASSES_1 - 1),
+                )
+            nc.vector.tensor_tensor(
+                out=z_sb[:, t, :].rearrange("p (u q e) -> p u q e", u=2, e=2),
+                in0=z_ps[:].rearrange("p (u e q) -> p u q e", u=2, e=2),
+                in1=b2_free[:].rearrange("p (u q e) -> p u q e", u=2, e=2),
+                op=ALU.add,
+            )
+            zt_ps = ps_1.tile([P, PACK, P], F32, tag="zt")
+            for j in range(PACK):
+                for g in range(PASSES_1):
+                    nc.tensor.matmul_mx(
+                        out=zt_ps[:, j, :],
+                        lhsT=w2_codes[:, g, j * P : (j + 1) * P].bitcast(FP8X4),
+                        lhsT_scale=w2_scales[:, g, j * P : (j + 1) * P],
+                        rhs=h_codes[:, t, g * P : (g + 1) * P].bitcast(FP8X4),
+                        rhs_scale=h_scales[:, t, g * P : (g + 1) * P],
+                        start=(g == 0),
+                        stop=(g == PASSES_1 - 1),
+                    )
+            z_grouped = stage.tile([P, P, PACK], BF16, align_bytes=64)
+            nc.vector.tensor_tensor(
+                out=z_grouped[:],
+                in0=zt_ps[:].rearrange("p j b -> p b j"),
+                in1=b2_part[:].unsqueeze(1).to_broadcast([P, P, PACK]),
+                op=ALU.add,
+            )
+            nc.vector.quantize_mx(
+                out=z_codes[:, t, :].bitcast(FP8X4),
+                scales=z_scales[:, t, :],
+                in_=z_grouped[:].rearrange("p b j -> p (b j)"),
+            )
+
+        prepare_chunk(0)
+        for t in range(B_TILES):
+            quantise_h(t)
+        for t in range(B_TILES):
+            first_product(t)
+            if t % 2 == 1:
+                nc.sync.dma_start(out=z_view[:, t - 1 : t + 1, :], in_=z_sb[:, t - 1 : t + 1, :])
+
+        low10 = keep.tile([P, B_TILES, MODULES], F32)
+        sums = keep.tile([P, B_TILES, MODULES], F32)
+        for j in range(CHUNKS):
+            if j + 1 < CHUNKS:
+                prepare_chunk(j + 1)
+            for first in range(0, B_TILES, GROUP):
+                a10 = work.tile([P, GROUP, BANK], F32)
+                for i in range(GROUP):
+                    t = first + i
+                    bank = ps_s.tile([P, BANK], F32, tag="bank")
+                    nc.tensor.matmul_mx(
+                        out=bank[:],
+                        lhsT=z_codes[:, t, :].bitcast(FP8X4),
+                        lhsT_scale=z_scales[:, t, :],
+                        rhs=w_codes[:, j, :].bitcast(FP8X4),
+                        rhs_scale=w_scales[:, j, :],
+                        start=True,
+                        stop=True,
+                    )
+                    nc.vector.scalar_tensor_tensor(
+                        out=a10[:, i, :], in0=bank[:], scalar=BETA, in1=bias10[:, j, :], op0=ALU.mult, op1=ALU.add
+                    )
+                nc.vector.tensor_reduce(
+                    out=low10[:, first : first + GROUP, j * MODS : (j + 1) * MODS],
+                    in_=a10[:].rearrange("p i (c k) -> p i c k", k=HEADS),
+                    axis=AXIS.X,
+                    op=ALU.min,
+                )
+                for i in range(GROUP):
+                    t = first + i
+                    for c in range(MODS):
+                        m = j * MODS + c
+                        nc.scalar.activation(
+                            out=a10[:, i, c * HEADS : (c + 1) * HEADS],
+                            in_=a10[:, i, c * HEADS : (c + 1) * HEADS],
+                            func=ACT.Exp,
+                            bias=low10[:, t, m : m + 1],
+                            scale=-1.0,
+                            accum_out=sums[:, t, m : m + 1],
+                        )
+
+        log_sums = keep.tile([P, B_TILES * MODULES], F32)
+        nc.scalar.activation(out=log_sums[:], in_=sums[:].rearrange("p t c -> p (t c)"), func=ACT.Ln)
+        conf = keep.tile([P, B_TILES * MODULES], F32)
+        nc.vector.tensor_tensor(
+            out=conf[:], in0=low10[:].rearrange("p t c -> p (t c)"), in1=log_sums[:], op=ALU.subtract
+        )
+        nc.sync.dma_start(out=conf_view, in_=conf[:])

@@ -20,7 +20,9 @@ BANK = 512
 CHUNKS = MODULES * HEADS // BANK
 MODS = BANK // HEADS
 ROW_TILES = BANK // P
-GROUP = 4
+GROUP = 2
+SIDE_TILES = 2
+LAG = 2
 
 FLOPS = 2 * BATCH * HIDDEN * LATENT + 2 * BATCH * LATENT * MODULES * HEADS
 
@@ -31,67 +33,57 @@ def tile_ace_pa_kernel(tc, h_enc, enc_w2, enc_b2, clus_w, clus_b, out_0, out_1):
     z_view = out_0.rearrange("(p t) d -> p t d", t=B_TILES)
     conf_view = out_1.rearrange("(p t) c -> p (t c)", t=B_TILES)
     cw_view = clus_w.rearrange("c k d -> (c k) d").rearrange("(r p) d -> p r d", p=P)
+    cb_view = clus_b.rearrange("c k -> (c k)")
+    w2_view = enc_w2.rearrange("(w p e) d -> p w (e d)", w=2 * PASSES_1, e=2)
 
-    with tc.tile_pool(name="keep", bufs=1) as keep, tc.tile_pool(name="stage", bufs=2) as stage, tc.tile_pool(
-        name="work", bufs=3
-    ) as work, tc.psum_pool(name="ps_t", bufs=2) as ps_t, tc.psum_pool(name="ps_1", bufs=1) as ps_1, tc.psum_pool(
-        name="ps_s", bufs=4
-    ) as ps_s:
-        bias_rows = keep.tile([P, CHUNKS * BANK + LATENT], BF16)
-        nc.vector.memset(bias_rows[:].bitcast(F32), 0.0)
-        b2_words = keep.tile([P, P], F32)
-        nc.vector.memset(b2_words[:], 0.0)
-        nc.scalar.dma_start(out=bias_rows[0:1, 0 : CHUNKS * BANK], in_=clus_b.rearrange("c k -> (c k)").unsqueeze(0))
-        nc.scalar.dma_start(out=bias_rows[0:1, CHUNKS * BANK :], in_=enc_b2.unsqueeze(0))
-        nc.scalar.dma_start(out=b2_words[0:2, :], in_=enc_b2.bitcast(F32).rearrange("(u q) -> u q", u=2))
+    with tc.tile_pool(name="keep", bufs=1) as keep, tc.tile_pool(name="stage", bufs=4) as stage, tc.tile_pool(
+        name="work", bufs=5
+    ) as work, tc.psum_pool(name="ps_flip", bufs=2) as ps_flip, tc.psum_pool(name="ps_bank", bufs=6) as ps_bank:
+        ident = keep.tile([P, P], F32)
+        make_identity(nc, ident[:])
+        warm_in = keep.tile([P, 1], F32)
+        nc.vector.memset(warm_in[:], 0.0)
 
         w2_raw = keep.tile([P, 2 * PASSES_1, 2 * LATENT], BF16)
-        nc.sync.dma_start(out=w2_raw[:], in_=enc_w2.rearrange("(w p e) d -> p w (e d)", w=2 * PASSES_1, e=2))
         h_sb = keep.tile([P, B_TILES * HIDDEN], BF16)
-        for t in range(0, B_TILES, 2):
+        cw_sb = keep.tile([P, CHUNKS * ROW_TILES * LATENT], BF16)
+        h_words = h_sb[:].bitcast(F32)
+        cw_words = cw_sb[:].bitcast(F32)
+        cb_free = keep.tile([P, CHUNKS, BANK], BF16)
+        bias10 = keep.tile([P, CHUNKS, BANK], F32)
+        b2_free = keep.tile([P, LATENT], BF16)
+        b2_pairs = keep.tile([P, 2], F32)
+        b2_part = keep.tile([P, PACK], F32)
+        w2_grouped = keep.tile([P, PASSES_1, LATENT, PACK], BF16, align_bytes=64)
+        w2_codes = keep.tile([P, PASSES_1, LATENT], U32, align_bytes=64)
+        w2_scales = keep.tile([P, PASSES_1, LATENT], U8, align_bytes=64)
+        w_codes = keep.tile([P, CHUNKS, BANK], U32, align_bytes=64)
+        w_scales = keep.tile([P, CHUNKS, BANK], U8, align_bytes=64)
+        h_codes = keep.tile([P, B_TILES, PASSES_1 * P], U32, align_bytes=64)
+        h_scales = keep.tile([P, B_TILES, PASSES_1 * P], U8, align_bytes=64)
+        z_sb = keep.tile([P, B_TILES, LATENT], F32)
+        z_codes = keep.tile([P, B_TILES, P], U32, align_bytes=64)
+        z_scales = keep.tile([P, B_TILES, P], U8, align_bytes=64)
+        low10 = keep.tile([P, B_TILES, MODULES], F32)
+        sums = keep.tile([P, B_TILES, MODULES], F32)
+        grouped_of = {}
+        a10_of = {}
+
+        def load_h(t):
             nc.sync.dma_start(
                 out=h_sb[:, t * HIDDEN : (t + 2) * HIDDEN].rearrange("p (t k) -> p t k", t=2), in_=h_view[:, t : t + 2, :]
             )
-        cw_sb = keep.tile([P, CHUNKS * ROW_TILES * LATENT], BF16)
-        for j in range(CHUNKS):
+
+        def load_chunk(j):
             nc.sync.dma_start(
                 out=cw_sb[:, j * ROW_TILES * LATENT : (j + 1) * ROW_TILES * LATENT].rearrange(
                     "p (r d) -> p r d", r=ROW_TILES
                 ),
                 in_=cw_view[:, j * ROW_TILES : (j + 1) * ROW_TILES, :],
             )
-        h_words = h_sb[:].bitcast(F32)
-        cw_words = cw_sb[:].bitcast(F32)
+            nc.sync.dma_start(out=cb_free[:, j, :], in_=cb_view[j * BANK : (j + 1) * BANK].partition_broadcast(P))
 
-        ident = keep.tile([P, P], F32)
-        make_identity(nc, ident[:])
-        ones = keep.tile([P, P], BF16)
-        nc.vector.memset(ones[:], 1.0)
-        warm_in = keep.tile([P, 1], F32)
-        nc.vector.memset(warm_in[:], 0.0)
-        warm_out = keep.tile([P, 1], F32)
-        nc.scalar.activation(out=warm_out[:], in_=warm_in[:], func=ACT.Exp)
-
-        bias10 = keep.tile([P, CHUNKS, BANK], F32)
-        for j in range(CHUNKS):
-            spread = ps_s.tile([P, BANK], F32, tag="bank")
-            nc.tensor.matmul(spread[:], lhsT=ones[:], rhs=bias_rows[:, j * BANK : (j + 1) * BANK], start=True, stop=True)
-            nc.scalar.mul(out=bias10[:, j, :], in_=spread[:], mul=BETA)
-        b2_free = keep.tile([P, LATENT], F32)
-        spread = ps_s.tile([P, BANK], F32, tag="bank")
-        nc.tensor.matmul(spread[:], lhsT=ones[:], rhs=bias_rows[:, CHUNKS * BANK :], start=True, stop=True)
-        nc.scalar.copy(out=b2_free[:], in_=spread[:])
-        flipped = ps_t.tile([P, PACK, P], F32, tag="flip")
-        nc.tensor.transpose(flipped[:, 0, :], b2_words[:], ident[:])
-        b2_pairs = keep.tile([P, 2], F32)
-        nc.vector.tensor_copy(out=b2_pairs[:], in_=flipped[:, 0, 0:2])
-        b2_part = keep.tile([P, PACK], F32)
-        nc.vector.tensor_copy(out=b2_part[:], in_=b2_pairs[:].bitcast(BF16))
-
-        w2_grouped = keep.tile([P, PASSES_1, LATENT, PACK], BF16, align_bytes=64)
-        w2_codes = keep.tile([P, PASSES_1, LATENT], U32, align_bytes=64)
-        w2_scales = keep.tile([P, PASSES_1, LATENT], U8, align_bytes=64)
-        for g in range(PASSES_1):
+        def regroup_w2(g):
             for u in range(2):
                 nc.vector.tensor_copy(
                     out=w2_grouped[:, g, 256 * u : 256 * (u + 1), :].rearrange("p (e q) j -> p e q j", e=2),
@@ -99,72 +91,56 @@ def tile_ace_pa_kernel(tc, h_enc, enc_w2, enc_b2, clus_w, clus_b, out_0, out_1):
                     .rearrange("p w (e d) -> p (w e) d", e=2)[:, :, 256 * u : 256 * (u + 1)]
                     .rearrange("p j (q e) -> p e q j", e=2),
                 )
-        for g in range(PASSES_1):
+
+        def quantise_w2(g):
             nc.vector.quantize_mx(
                 out=w2_codes[:, g, :].bitcast(FP8X4),
                 scales=w2_scales[:, g, :],
                 in_=w2_grouped[:, g, :, :].rearrange("p d j -> p (d j)"),
             )
 
-        w_codes = keep.tile([P, CHUNKS, BANK], U32, align_bytes=64)
-        w_scales = keep.tile([P, CHUNKS, BANK], U8, align_bytes=64)
-
-        def prepare_chunk(j):
+        def flip_chunk(j):
+            nc.gpsimd.tensor_scalar(
+                out=bias10[:, j, :], in0=cb_free[:, j, :], scalar1=BETA, scalar2=0.0, op0=ALU.mult, op1=ALU.add
+            )
             w_grouped = stage.tile([P, BANK * PACK], BF16, align_bytes=64)
+            grouped_of["w", j] = w_grouped
             for half in range(2):
-                flip_w = ps_t.tile([P, PACK, P], F32, tag="flip")
+                flip_w = ps_flip.tile([P, PACK, P], F32, tag="flip")
                 for u in range(2):
                     for rr in range(2):
                         r = j * ROW_TILES + 2 * half + rr
                         nc.tensor.transpose(
-                            flip_w[:, 2 * u + rr, :],
-                            cw_words[:, r * 256 + u * P : r * 256 + (u + 1) * P],
-                            ident[:],
+                            flip_w[:, 2 * u + rr, :], cw_words[:, r * 256 + u * P : r * 256 + (u + 1) * P], ident[:]
                         )
                 nc.scalar.copy(
                     out=w_grouped[:, half * 1024 : (half + 1) * 1024].bitcast(F32).rearrange("p (n u) -> p n u", u=2),
                     in_=flip_w[:].rearrange("p (u r) q -> p (r q) u", u=2),
                 )
-            nc.vector.quantize_mx(out=w_codes[:, j, :].bitcast(FP8X4), scales=w_scales[:, j, :], in_=w_grouped[:])
 
-        h_codes = keep.tile([P, B_TILES, PASSES_1 * P], U32, align_bytes=64)
-        h_scales = keep.tile([P, B_TILES, PASSES_1 * P], U8, align_bytes=64)
-        z_sb = keep.tile([P, B_TILES, LATENT], F32)
-        z_codes = keep.tile([P, B_TILES, P], U32, align_bytes=64)
-        z_scales = keep.tile([P, B_TILES, P], U8, align_bytes=64)
+        def quantise_chunk(j):
+            nc.vector.quantize_mx(
+                out=w_codes[:, j, :].bitcast(FP8X4), scales=w_scales[:, j, :], in_=grouped_of["w", j][:]
+            )
 
-        def quantise_h(t):
-            flip_h = ps_t.tile([P, PACK, P], F32, tag="flip")
+        def flip_h(t):
+            flip = ps_flip.tile([P, PACK, P], F32, tag="flip")
             for w in range(2 * PASSES_1):
-                nc.tensor.transpose(
-                    flip_h[:, w, :], h_words[:, t * 512 + w * P : t * 512 + (w + 1) * P], ident[:]
-                )
+                nc.tensor.transpose(flip[:, w, :], h_words[:, t * 512 + w * P : t * 512 + (w + 1) * P], ident[:])
             h_grouped = stage.tile([P, PASSES_1 * P * PACK], BF16, align_bytes=64)
+            grouped_of["h", t] = h_grouped
             nc.scalar.copy(
                 out=h_grouped[:].bitcast(F32).rearrange("p (g b u) -> p g b u", g=PASSES_1, u=2),
-                in_=flip_h[:].rearrange("p (g u) b -> p g b u", u=2),
+                in_=flip[:].rearrange("p (g u) b -> p g b u", u=2),
             )
-            nc.vector.quantize_mx(out=h_codes[:, t, :].bitcast(FP8X4), scales=h_scales[:, t, :], in_=h_grouped[:])
+
+        def quantise_h(t):
+            nc.vector.quantize_mx(
+                out=h_codes[:, t, :].bitcast(FP8X4), scales=h_scales[:, t, :], in_=grouped_of["h", t][:]
+            )
 
         def first_product(t):
-            z_ps = ps_1.tile([P, LATENT], F32, tag="z")
-            for g in range(PASSES_1):
-                nc.tensor.matmul_mx(
-                    out=z_ps[:],
-                    lhsT=h_codes[:, t, g * P : (g + 1) * P].bitcast(FP8X4),
-                    lhsT_scale=h_scales[:, t, g * P : (g + 1) * P],
-                    rhs=w2_codes[:, g, :].bitcast(FP8X4),
-                    rhs_scale=w2_scales[:, g, :],
-                    start=(g == 0),
-                    stop=(g == PASSES_1 - 1),
-                )
-            nc.vector.tensor_tensor(
-                out=z_sb[:, t, :].rearrange("p (u q e) -> p u q e", u=2, e=2),
-                in0=z_ps[:].rearrange("p (u e q) -> p u q e", u=2, e=2),
-                in1=b2_free[:].rearrange("p (u q e) -> p u q e", u=2, e=2),
-                op=ALU.add,
-            )
-            zt_ps = ps_1.tile([P, PACK, P], F32, tag="zt")
+            zt_ps = ps_bank.tile([P, PACK, P], F32, tag="bank")
             for j in range(PACK):
                 for g in range(PASSES_1):
                     nc.tensor.matmul_mx(
@@ -176,11 +152,28 @@ def tile_ace_pa_kernel(tc, h_enc, enc_w2, enc_b2, clus_w, clus_b, out_0, out_1):
                         start=(g == 0),
                         stop=(g == PASSES_1 - 1),
                     )
+            z_ps = ps_bank.tile([P, LATENT], F32, tag="bank")
+            for g in range(PASSES_1):
+                nc.tensor.matmul_mx(
+                    out=z_ps[:],
+                    lhsT=h_codes[:, t, g * P : (g + 1) * P].bitcast(FP8X4),
+                    lhsT_scale=h_scales[:, t, g * P : (g + 1) * P],
+                    rhs=w2_codes[:, g, :].bitcast(FP8X4),
+                    rhs_scale=w2_scales[:, g, :],
+                    start=(g == 0),
+                    stop=(g == PASSES_1 - 1),
+                )
             z_grouped = stage.tile([P, P, PACK], BF16, align_bytes=64)
             nc.vector.tensor_tensor(
                 out=z_grouped[:],
                 in0=zt_ps[:].rearrange("p j b -> p b j"),
                 in1=b2_part[:].unsqueeze(1).to_broadcast([P, P, PACK]),
+                op=ALU.add,
+            )
+            nc.vector.tensor_tensor(
+                out=z_sb[:, t, :].rearrange("p (u q e) -> p u q e", u=2, e=2),
+                in0=z_ps[:].rearrange("p (u e q) -> p u q e", u=2, e=2),
+                in1=b2_free[:].rearrange("p (u q e) -> p u q e", u=2, e=2),
                 op=ALU.add,
             )
             nc.vector.quantize_mx(
@@ -189,59 +182,102 @@ def tile_ace_pa_kernel(tc, h_enc, enc_w2, enc_b2, clus_w, clus_b, out_0, out_1):
                 in_=z_grouped[:].rearrange("p b j -> p (b j)"),
             )
 
-        prepare_chunk(0)
-        for t in range(B_TILES):
-            quantise_h(t)
-        for t in range(B_TILES):
-            first_product(t)
-            if t % 2 == 1:
-                nc.sync.dma_start(out=z_view[:, t - 1 : t + 1, :], in_=z_sb[:, t - 1 : t + 1, :])
-
-        low10 = keep.tile([P, B_TILES, MODULES], F32)
-        sums = keep.tile([P, B_TILES, MODULES], F32)
-        for j in range(CHUNKS):
-            if j + 1 < CHUNKS:
-                prepare_chunk(j + 1)
-            for first in range(0, B_TILES, GROUP):
-                a10 = work.tile([P, GROUP, BANK], F32)
-                for i in range(GROUP):
-                    t = first + i
-                    bank = ps_s.tile([P, BANK], F32, tag="bank")
-                    nc.tensor.matmul_mx(
-                        out=bank[:],
-                        lhsT=z_codes[:, t, :].bitcast(FP8X4),
-                        lhsT_scale=z_scales[:, t, :],
-                        rhs=w_codes[:, j, :].bitcast(FP8X4),
-                        rhs_scale=w_scales[:, j, :],
-                        start=True,
-                        stop=True,
-                    )
+        def scores(j, first):
+            a10 = work.tile([P, GROUP, BANK], F32)
+            a10_of[j, first] = a10
+            for i in range(GROUP):
+                t = first + i
+                bank = ps_bank.tile([P, BANK], F32, tag="bank")
+                nc.tensor.matmul_mx(
+                    out=bank[:],
+                    lhsT=z_codes[:, t, :].bitcast(FP8X4),
+                    lhsT_scale=z_scales[:, t, :],
+                    rhs=w_codes[:, j, :].bitcast(FP8X4),
+                    rhs_scale=w_scales[:, j, :],
+                    start=True,
+                    stop=True,
+                )
+                if t >= B_TILES - SIDE_TILES:
+                    nc.scalar.mul(out=a10[:, i, :], in_=bank[:], mul=BETA)
+                    nc.gpsimd.tensor_tensor(out=a10[:, i, :], in0=a10[:, i, :], in1=bias10[:, j, :], op=ALU.add)
+                else:
                     nc.vector.scalar_tensor_tensor(
                         out=a10[:, i, :], in0=bank[:], scalar=BETA, in1=bias10[:, j, :], op0=ALU.mult, op1=ALU.add
                     )
-                nc.vector.tensor_reduce(
-                    out=low10[:, first : first + GROUP, j * MODS : (j + 1) * MODS],
-                    in_=a10[:].rearrange("p i (c k) -> p i c k", k=HEADS),
-                    axis=AXIS.X,
-                    op=ALU.min,
-                )
-                for i in range(GROUP):
-                    t = first + i
-                    for c in range(MODS):
-                        m = j * MODS + c
-                        nc.scalar.activation(
-                            out=a10[:, i, c * HEADS : (c + 1) * HEADS],
-                            in_=a10[:, i, c * HEADS : (c + 1) * HEADS],
-                            func=ACT.Exp,
-                            bias=low10[:, t, m : m + 1],
-                            scale=-1.0,
-                            accum_out=sums[:, t, m : m + 1],
-                        )
 
-        log_sums = keep.tile([P, B_TILES * MODULES], F32)
-        nc.scalar.activation(out=log_sums[:], in_=sums[:].rearrange("p t c -> p (t c)"), func=ACT.Ln)
-        conf = keep.tile([P, B_TILES * MODULES], F32)
-        nc.vector.tensor_tensor(
-            out=conf[:], in0=low10[:].rearrange("p t c -> p (t c)"), in1=log_sums[:], op=ALU.subtract
-        )
-        nc.sync.dma_start(out=conf_view, in_=conf[:])
+        def soft_min(j, first):
+            a10 = a10_of[j, first]
+            nc.vector.tensor_reduce(
+                out=low10[:, first : first + GROUP, j * MODS : (j + 1) * MODS],
+                in_=a10[:].rearrange("p i (c k) -> p i c k", k=HEADS),
+                axis=AXIS.X,
+                op=ALU.min,
+            )
+            for i in range(GROUP):
+                for c in range(MODS):
+                    m = j * MODS + c
+                    nc.scalar.activation(
+                        out=a10[:, i, c * HEADS : (c + 1) * HEADS],
+                        in_=a10[:, i, c * HEADS : (c + 1) * HEADS],
+                        func=ACT.Exp,
+                        bias=low10[:, first + i, m : m + 1],
+                        scale=-1.0,
+                        accum_out=sums[:, first + i, m : m + 1],
+                    )
+
+        with tc.manual_schedule():
+            nc.sync.dma_start(out=b2_pairs[:], in_=enc_b2.bitcast(F32).rearrange("(u q) -> q u", u=2))
+            nc.sync.dma_start(out=b2_free[:], in_=enc_b2.partition_broadcast(P))
+            for g in range(PASSES_1):
+                nc.sync.dma_start(out=w2_raw[:, 2 * g : 2 * g + 2, :], in_=w2_view[:, 2 * g : 2 * g + 2, :])
+            load_h(0)
+            load_h(2)
+            load_chunk(0)
+            load_h(4)
+            load_h(6)
+            for j in range(1, CHUNKS):
+                load_chunk(j)
+            warm_out = keep.tile([P, 1], F32)
+            nc.scalar.activation(out=warm_out[:], in_=warm_in[:], func=ACT.Exp)
+
+            nc.vector.tensor_copy(out=b2_part[:], in_=b2_pairs[:].bitcast(BF16))
+            for g in range(PASSES_1):
+                regroup_w2(g)
+            for g in range(PASSES_1):
+                quantise_w2(g)
+            for t in range(0, B_TILES, 2):
+                flip_h(t)
+                flip_h(t + 1)
+                if t == 2:
+                    flip_chunk(0)
+                quantise_h(t)
+                quantise_h(t + 1)
+                if t >= 2:
+                    first_product(t - 2)
+                    first_product(t - 1)
+                    nc.sync.dma_start(out=z_view[:, t - 2 : t, :], in_=z_sb[:, t - 2 : t, :])
+            quantise_chunk(0)
+            first_product(B_TILES - 2)
+            first_product(B_TILES - 1)
+            nc.sync.dma_start(out=z_view[:, B_TILES - 2 :, :], in_=z_sb[:, B_TILES - 2 :, :])
+
+            firsts = list(reversed(range(0, B_TILES, GROUP)))
+            groups = [(j, first) for j in range(CHUNKS) for first in firsts]
+            for n, (j, first) in enumerate(groups):
+                scores(j, first)
+                if first == firsts[0] and j + 1 < CHUNKS:
+                    flip_chunk(j + 1)
+                if first == firsts[1] and j + 1 < CHUNKS:
+                    quantise_chunk(j + 1)
+                if n >= LAG:
+                    soft_min(*groups[n - LAG])
+            for n in range(len(groups) - LAG, len(groups)):
+                soft_min(*groups[n])
+
+            log_sums = keep.tile([P, B_TILES * MODULES], F32)
+            nc.scalar.activation(out=log_sums[:], in_=sums[:].rearrange("p t c -> p (t c)"), func=ACT.Ln)
+            conf = keep.tile([P, B_TILES * MODULES], F32)
+            nc.vector.tensor_tensor(
+                out=conf[:], in0=low10[:].rearrange("p t c -> p (t c)"), in1=log_sums[:], op=ALU.subtract
+            )
+            nc.sync.dma_start(out=conf_view, in_=conf[:])

@@ -21,8 +21,6 @@ CHUNKS = MODULES * HEADS // BANK
 MODS = BANK // HEADS
 ROW_TILES = BANK // P
 GROUP = 2
-SIDE_TILES = 2
-LAG = 2
 
 FLOPS = 2 * BATCH * HIDDEN * LATENT + 2 * BATCH * LATENT * MODULES * HEADS
 
@@ -139,7 +137,7 @@ def tile_ace_pa_kernel(tc, h_enc, enc_w2, enc_b2, clus_w, clus_b, out_0, out_1):
                 out=h_codes[:, t, :].bitcast(FP8X4), scales=h_scales[:, t, :], in_=grouped_of["h", t][:]
             )
 
-        def first_product(t):
+        def quantise_z(t):
             zt_ps = ps_bank.tile([P, PACK, P], F32, tag="bank")
             for j in range(PACK):
                 for g in range(PASSES_1):
@@ -152,6 +150,23 @@ def tile_ace_pa_kernel(tc, h_enc, enc_w2, enc_b2, clus_w, clus_b, out_0, out_1):
                         start=(g == 0),
                         stop=(g == PASSES_1 - 1),
                     )
+            z_grouped = stage.tile([P, P, PACK], BF16, align_bytes=64)
+            grouped_of["z", t] = z_grouped
+            nc.vector.tensor_tensor(
+                out=z_grouped[:],
+                in0=zt_ps[:].rearrange("p j b -> p b j"),
+                in1=b2_part[:].unsqueeze(1).to_broadcast([P, P, PACK]),
+                op=ALU.add,
+            )
+
+        def quantise_z_codes(t):
+            nc.vector.quantize_mx(
+                out=z_codes[:, t, :].bitcast(FP8X4),
+                scales=z_scales[:, t, :],
+                in_=grouped_of["z", t][:].rearrange("p b j -> p (b j)"),
+            )
+
+        def output_z(t):
             z_ps = ps_bank.tile([P, LATENT], F32, tag="bank")
             for g in range(PASSES_1):
                 nc.tensor.matmul_mx(
@@ -163,23 +178,11 @@ def tile_ace_pa_kernel(tc, h_enc, enc_w2, enc_b2, clus_w, clus_b, out_0, out_1):
                     start=(g == 0),
                     stop=(g == PASSES_1 - 1),
                 )
-            z_grouped = stage.tile([P, P, PACK], BF16, align_bytes=64)
-            nc.vector.tensor_tensor(
-                out=z_grouped[:],
-                in0=zt_ps[:].rearrange("p j b -> p b j"),
-                in1=b2_part[:].unsqueeze(1).to_broadcast([P, P, PACK]),
-                op=ALU.add,
-            )
             nc.vector.tensor_tensor(
                 out=z_sb[:, t, :].rearrange("p (u q e) -> p u q e", u=2, e=2),
                 in0=z_ps[:].rearrange("p (u e q) -> p u q e", u=2, e=2),
                 in1=b2_free[:].rearrange("p (u q e) -> p u q e", u=2, e=2),
                 op=ALU.add,
-            )
-            nc.vector.quantize_mx(
-                out=z_codes[:, t, :].bitcast(FP8X4),
-                scales=z_scales[:, t, :],
-                in_=z_grouped[:].rearrange("p b j -> p (b j)"),
             )
 
         def scores(j, first):
@@ -197,13 +200,9 @@ def tile_ace_pa_kernel(tc, h_enc, enc_w2, enc_b2, clus_w, clus_b, out_0, out_1):
                     start=True,
                     stop=True,
                 )
-                if t >= B_TILES - SIDE_TILES:
-                    nc.scalar.mul(out=a10[:, i, :], in_=bank[:], mul=BETA)
-                    nc.gpsimd.tensor_tensor(out=a10[:, i, :], in0=a10[:, i, :], in1=bias10[:, j, :], op=ALU.add)
-                else:
-                    nc.vector.scalar_tensor_tensor(
-                        out=a10[:, i, :], in0=bank[:], scalar=BETA, in1=bias10[:, j, :], op0=ALU.mult, op1=ALU.add
-                    )
+                nc.vector.scalar_tensor_tensor(
+                    out=a10[:, i, :], in0=bank[:], scalar=BETA, in1=bias10[:, j, :], op0=ALU.mult, op1=ALU.add
+                )
 
         def soft_min(j, first):
             a10 = a10_of[j, first]
@@ -226,53 +225,58 @@ def tile_ace_pa_kernel(tc, h_enc, enc_w2, enc_b2, clus_w, clus_b, out_0, out_1):
                     )
 
         with tc.manual_schedule():
-            nc.sync.dma_start(out=b2_pairs[:], in_=enc_b2.bitcast(F32).rearrange("(u q) -> q u", u=2))
-            nc.sync.dma_start(out=b2_free[:], in_=enc_b2.partition_broadcast(P))
             for g in range(PASSES_1):
                 nc.sync.dma_start(out=w2_raw[:, 2 * g : 2 * g + 2, :], in_=w2_view[:, 2 * g : 2 * g + 2, :])
             load_h(0)
-            load_h(2)
+            nc.sync.dma_start(out=b2_pairs[:], in_=enc_b2.bitcast(F32).rearrange("(u q) -> q u", u=2))
+            nc.sync.dma_start(out=b2_free[:], in_=enc_b2.partition_broadcast(P))
             load_chunk(0)
-            load_h(4)
-            load_h(6)
+            for t in range(2, B_TILES, 2):
+                load_h(t)
             for j in range(1, CHUNKS):
                 load_chunk(j)
             warm_out = keep.tile([P, 1], F32)
             nc.scalar.activation(out=warm_out[:], in_=warm_in[:], func=ACT.Exp)
 
-            nc.vector.tensor_copy(out=b2_part[:], in_=b2_pairs[:].bitcast(BF16))
             for g in range(PASSES_1):
                 regroup_w2(g)
             for g in range(PASSES_1):
                 quantise_w2(g)
-            for t in range(0, B_TILES, 2):
+            nc.vector.tensor_copy(out=b2_part[:], in_=b2_pairs[:].bitcast(BF16))
+            for t in range(GROUP):
                 flip_h(t)
-                flip_h(t + 1)
-                if t == 2:
-                    flip_chunk(0)
+            flip_chunk(0)
+            for t in range(GROUP):
                 quantise_h(t)
-                quantise_h(t + 1)
-                if t >= 2:
-                    first_product(t - 2)
-                    first_product(t - 1)
-                    nc.sync.dma_start(out=z_view[:, t - 2 : t, :], in_=z_sb[:, t - 2 : t, :])
             quantise_chunk(0)
-            first_product(B_TILES - 2)
-            first_product(B_TILES - 1)
-            nc.sync.dma_start(out=z_view[:, B_TILES - 2 :, :], in_=z_sb[:, B_TILES - 2 :, :])
 
-            firsts = list(reversed(range(0, B_TILES, GROUP)))
-            groups = [(j, first) for j in range(CHUNKS) for first in firsts]
+            groups = [(j, first) for j in range(CHUNKS) for first in range(0, B_TILES, GROUP)]
             for n, (j, first) in enumerate(groups):
+                if j == 0:
+                    later = range(first + GROUP, min(first + 2 * GROUP, B_TILES))
+                    for t in range(first, first + GROUP):
+                        quantise_z(t)
+                    for t in later:
+                        flip_h(t)
+                    for t in later:
+                        quantise_h(t)
+                    for t in range(first, first + GROUP):
+                        quantise_z_codes(t)
+                    if n > 0:
+                        soft_min(*groups[n - 1])
                 scores(j, first)
-                if first == firsts[0] and j + 1 < CHUNKS:
+                if first == 0 and j + 1 < CHUNKS:
                     flip_chunk(j + 1)
-                if first == firsts[1] and j + 1 < CHUNKS:
+                if first == GROUP and j + 1 < CHUNKS:
                     quantise_chunk(j + 1)
-                if n >= LAG:
-                    soft_min(*groups[n - LAG])
-            for n in range(len(groups) - LAG, len(groups)):
-                soft_min(*groups[n])
+                if j > 0:
+                    soft_min(*groups[n - 1])
+            soft_min(*groups[-1])
+
+            for t in range(B_TILES):
+                output_z(t)
+                if t % 2 == 1:
+                    nc.sync.dma_start(out=z_view[:, t - 1 : t + 1, :], in_=z_sb[:, t - 1 : t + 1, :])
 
             log_sums = keep.tile([P, B_TILES * MODULES], F32)
             nc.scalar.activation(out=log_sums[:], in_=sums[:].rearrange("p t c -> p (t c)"), func=ACT.Ln)

@@ -40,7 +40,7 @@ def tile_ace_pa_kernel(tc, h_enc, enc_w2, enc_b2, clus_w, clus_b, out_0, out_1):
         ident = keep.tile([P, P], F32)
         make_identity(nc, ident[:])
         warm_in = keep.tile([P, 1], F32)
-        nc.vector.memset(warm_in[:], 0.0)
+        nc.vector.memset(warm_in[:], 1.0)
 
         w2_raw = keep.tile([P, 2 * PASSES_1, 2 * LATENT], BF16)
         h_sb = keep.tile([P, B_TILES * HIDDEN], BF16)
@@ -79,6 +79,8 @@ def tile_ace_pa_kernel(tc, h_enc, enc_w2, enc_b2, clus_w, clus_b, out_0, out_1):
                 ),
                 in_=cw_view[:, j * ROW_TILES : (j + 1) * ROW_TILES, :],
             )
+
+        def load_bias(j):
             nc.sync.dma_start(out=cb_free[:, j, :], in_=cb_view[j * BANK : (j + 1) * BANK].partition_broadcast(P))
 
         def regroup_w2(g):
@@ -225,18 +227,21 @@ def tile_ace_pa_kernel(tc, h_enc, enc_w2, enc_b2, clus_w, clus_b, out_0, out_1):
                     )
 
         with tc.manual_schedule():
+            nc.scalar.dma_start(out=b2_pairs[:], in_=enc_b2.bitcast(F32).rearrange("(u q) -> q u", u=2))
             for g in range(PASSES_1):
                 nc.sync.dma_start(out=w2_raw[:, 2 * g : 2 * g + 2, :], in_=w2_view[:, 2 * g : 2 * g + 2, :])
             load_h(0)
-            nc.sync.dma_start(out=b2_pairs[:], in_=enc_b2.bitcast(F32).rearrange("(u q) -> q u", u=2))
-            nc.sync.dma_start(out=b2_free[:], in_=enc_b2.partition_broadcast(P))
             load_chunk(0)
+            load_bias(0)
             for t in range(2, B_TILES, 2):
                 load_h(t)
             for j in range(1, CHUNKS):
                 load_chunk(j)
+            for j in range(1, CHUNKS):
+                load_bias(j)
+            nc.sync.dma_start(out=b2_free[:], in_=enc_b2.partition_broadcast(P))
             warm_out = keep.tile([P, 1], F32)
-            nc.scalar.activation(out=warm_out[:], in_=warm_in[:], func=ACT.Exp)
+            nc.scalar.activation(out=warm_out[:], in_=warm_in[:], func=ACT.Ln)
 
             for g in range(PASSES_1):
                 regroup_w2(g)

@@ -35,8 +35,8 @@ def tile_ace_pa_kernel(tc, h_enc, enc_w2, enc_b2, clus_w, clus_b, out_0, out_1):
     w2_view = enc_w2.rearrange("(w p e) d -> p w (e d)", w=2 * PASSES_1, e=2)
 
     with tc.tile_pool(name="keep", bufs=1) as keep, tc.tile_pool(name="stage", bufs=4) as stage, tc.tile_pool(
-        name="work", bufs=5
-    ) as work, tc.psum_pool(name="ps_flip", bufs=2) as ps_flip, tc.psum_pool(name="ps_bank", bufs=6) as ps_bank:
+        name="chunks", bufs=CHUNKS
+    ) as chunks, tc.tile_pool(name="work", bufs=5) as work, tc.psum_pool(name="ps_flip", bufs=2) as ps_flip, tc.psum_pool(name="ps_bank", bufs=6) as ps_bank:
         ident = keep.tile([P, P], F32)
         make_identity(nc, ident[:])
         warm_in = keep.tile([P, 1], F32)
@@ -103,7 +103,7 @@ def tile_ace_pa_kernel(tc, h_enc, enc_w2, enc_b2, clus_w, clus_b, out_0, out_1):
             nc.gpsimd.tensor_scalar(
                 out=bias10[:, j, :], in0=cb_free[:, j, :], scalar1=BETA, scalar2=0.0, op0=ALU.mult, op1=ALU.add
             )
-            w_grouped = stage.tile([P, BANK * PACK], BF16, align_bytes=64)
+            w_grouped = chunks.tile([P, BANK * PACK], BF16, align_bytes=64)
             grouped_of["w", j] = w_grouped
             for half in range(2):
                 flip_w = ps_flip.tile([P, PACK, P], F32, tag="flip")
@@ -241,7 +241,7 @@ def tile_ace_pa_kernel(tc, h_enc, enc_w2, enc_b2, clus_w, clus_b, out_0, out_1):
                 load_bias(j)
             nc.sync.dma_start(out=b2_free[:], in_=enc_b2.partition_broadcast(P))
             warm_out = keep.tile([P, 1], F32)
-            nc.scalar.activation(out=warm_out[:], in_=warm_in[:], func=ACT.Ln)
+            nc.scalar.activation(out=warm_out[:], in_=warm_in[:], func=ACT.Exp)
 
             for g in range(PASSES_1):
                 regroup_w2(g)
@@ -263,6 +263,8 @@ def tile_ace_pa_kernel(tc, h_enc, enc_w2, enc_b2, clus_w, clus_b, out_0, out_1):
                         quantise_z(t)
                     for t in later:
                         flip_h(t)
+                    if n > 0:
+                        flip_chunk(n)
                     for t in later:
                         quantise_h(t)
                     for t in range(first, first + GROUP):
@@ -270,8 +272,8 @@ def tile_ace_pa_kernel(tc, h_enc, enc_w2, enc_b2, clus_w, clus_b, out_0, out_1):
                     if n > 0:
                         soft_min(*groups[n - 1])
                 scores(j, first)
-                if first == 0 and j + 1 < CHUNKS:
-                    flip_chunk(j + 1)
+                if j > 0 and n < CHUNKS:
+                    flip_chunk(n)
                 if first == GROUP and j + 1 < CHUNKS:
                     quantise_chunk(j + 1)
                 if j > 0:

@@ -188,6 +188,7 @@ def tile_ace_pa_kernel(tc, h_enc, enc_w2, enc_b2, clus_w, clus_b, out_0, out_1):
             )
 
         def scores(j, first):
+            split = first >= B_TILES // 2
             a10 = work.tile([P, GROUP, BANK], F32)
             a10_of[j, first] = a10
             for i in range(GROUP):
@@ -202,9 +203,13 @@ def tile_ace_pa_kernel(tc, h_enc, enc_w2, enc_b2, clus_w, clus_b, out_0, out_1):
                     start=True,
                     stop=True,
                 )
-                nc.vector.scalar_tensor_tensor(
-                    out=a10[:, i, :], in0=bank[:], scalar=BETA, in1=bias10[:, j, :], op0=ALU.mult, op1=ALU.add
-                )
+                if split and i == GROUP - 1:
+                    nc.scalar.activation(out=a10[:, i, :], in_=bank[:], func=ACT.Copy, scale=BETA)
+                    nc.gpsimd.tensor_tensor(out=a10[:, i, :], in0=a10[:, i, :], in1=bias10[:, j, :], op=ALU.add)
+                else:
+                    nc.vector.scalar_tensor_tensor(
+                        out=a10[:, i, :], in0=bank[:], scalar=BETA, in1=bias10[:, j, :], op0=ALU.mult, op1=ALU.add
+                    )
 
         def soft_min(j, first):
             a10 = a10_of[j, first]

@@ -21,6 +21,8 @@ CHUNKS = MODULES * HEADS // BANK
 MODS = BANK // HEADS
 ROW_TILES = BANK // P
 GROUP = 2
+PAIRS = B_TILES // GROUP
+SHARED = range(5, 32, 4)
 
 FLOPS = 2 * BATCH * HIDDEN * LATENT + 2 * BATCH * LATENT * MODULES * HEADS
 
@@ -35,8 +37,8 @@ def tile_ace_pa_kernel(tc, h_enc, enc_w2, enc_b2, clus_w, clus_b, out_0, out_1):
     w2_view = enc_w2.rearrange("(w p e) d -> p w (e d)", w=2 * PASSES_1, e=2)
 
     with tc.tile_pool(name="keep", bufs=1) as keep, tc.tile_pool(name="stage", bufs=4) as stage, tc.tile_pool(
-        name="chunks", bufs=CHUNKS
-    ) as chunks, tc.tile_pool(name="work", bufs=5) as work, tc.psum_pool(name="ps_flip", bufs=2) as ps_flip, tc.psum_pool(name="ps_bank", bufs=6) as ps_bank:
+        name="chunks", bufs=8
+    ) as chunks, tc.tile_pool(name="work", bufs=8) as work, tc.psum_pool(name="ps_flip", bufs=4) as ps_flip, tc.psum_pool(name="ps_bank", bufs=4) as ps_bank:
         ident = keep.tile([P, P], F32)
         make_identity(nc, ident[:])
         warm_in = keep.tile([P, 1], F32)
@@ -67,10 +69,14 @@ def tile_ace_pa_kernel(tc, h_enc, enc_w2, enc_b2, clus_w, clus_b, out_0, out_1):
         grouped_of = {}
         a10_of = {}
 
-        def load_h(t):
+        def load_h(t, count):
             nc.sync.dma_start(
-                out=h_sb[:, t * HIDDEN : (t + 2) * HIDDEN].rearrange("p (t k) -> p t k", t=2), in_=h_view[:, t : t + 2, :]
+                out=h_sb[:, t * HIDDEN : (t + count) * HIDDEN].rearrange("p (t k) -> p t k", t=count),
+                in_=h_view[:, t : t + count, :],
             )
+
+        def load_w2(g):
+            nc.sync.dma_start(out=w2_raw[:, 2 * g : 2 * g + 2, :], in_=w2_view[:, 2 * g : 2 * g + 2, :])
 
         def load_chunk(j):
             nc.sync.dma_start(
@@ -82,6 +88,11 @@ def tile_ace_pa_kernel(tc, h_enc, enc_w2, enc_b2, clus_w, clus_b, out_0, out_1):
 
         def load_bias(j):
             nc.sync.dma_start(out=cb_free[:, j, :], in_=cb_view[j * BANK : (j + 1) * BANK].partition_broadcast(P))
+
+        def scale_bias(j):
+            nc.gpsimd.tensor_scalar(
+                out=bias10[:, j, :], in0=cb_free[:, j, :], scalar1=BETA, scalar2=0.0, op0=ALU.mult, op1=ALU.add
+            )
 
         def regroup_w2(g):
             for u in range(2):
@@ -99,24 +110,22 @@ def tile_ace_pa_kernel(tc, h_enc, enc_w2, enc_b2, clus_w, clus_b, out_0, out_1):
                 in_=w2_grouped[:, g, :, :].rearrange("p d j -> p (d j)"),
             )
 
-        def flip_chunk(j):
-            nc.gpsimd.tensor_scalar(
-                out=bias10[:, j, :], in0=cb_free[:, j, :], scalar1=BETA, scalar2=0.0, op0=ALU.mult, op1=ALU.add
+        def flip_chunk(j, half):
+            if half == 0:
+                w_tile = chunks.tile([P, BANK * PACK], BF16, align_bytes=64)
+                grouped_of["w", j] = w_tile
+            w_grouped = grouped_of["w", j]
+            flip_w = ps_flip.tile([P, PACK, P], F32, tag="flip")
+            for u in range(2):
+                for rr in range(2):
+                    r = j * ROW_TILES + 2 * half + rr
+                    nc.tensor.transpose(
+                        flip_w[:, 2 * u + rr, :], cw_words[:, r * 256 + u * P : r * 256 + (u + 1) * P], ident[:]
+                    )
+            nc.scalar.copy(
+                out=w_grouped[:, half * 1024 : (half + 1) * 1024].bitcast(F32).rearrange("p (n u) -> p n u", u=2),
+                in_=flip_w[:].rearrange("p (u r) q -> p (r q) u", u=2),
             )
-            w_grouped = chunks.tile([P, BANK * PACK], BF16, align_bytes=64)
-            grouped_of["w", j] = w_grouped
-            for half in range(2):
-                flip_w = ps_flip.tile([P, PACK, P], F32, tag="flip")
-                for u in range(2):
-                    for rr in range(2):
-                        r = j * ROW_TILES + 2 * half + rr
-                        nc.tensor.transpose(
-                            flip_w[:, 2 * u + rr, :], cw_words[:, r * 256 + u * P : r * 256 + (u + 1) * P], ident[:]
-                        )
-                nc.scalar.copy(
-                    out=w_grouped[:, half * 1024 : (half + 1) * 1024].bitcast(F32).rearrange("p (n u) -> p n u", u=2),
-                    in_=flip_w[:].rearrange("p (u r) q -> p (r q) u", u=2),
-                )
 
         def quantise_chunk(j):
             nc.vector.quantize_mx(
@@ -139,7 +148,7 @@ def tile_ace_pa_kernel(tc, h_enc, enc_w2, enc_b2, clus_w, clus_b, out_0, out_1):
                 out=h_codes[:, t, :].bitcast(FP8X4), scales=h_scales[:, t, :], in_=grouped_of["h", t][:]
             )
 
-        def quantise_z(t):
+        def make_zt(t):
             zt_ps = ps_bank.tile([P, PACK, P], F32, tag="bank")
             for j in range(PACK):
                 for g in range(PASSES_1):
@@ -161,13 +170,6 @@ def tile_ace_pa_kernel(tc, h_enc, enc_w2, enc_b2, clus_w, clus_b, out_0, out_1):
                 op=ALU.add,
             )
 
-        def quantise_z_codes(t):
-            nc.vector.quantize_mx(
-                out=z_codes[:, t, :].bitcast(FP8X4),
-                scales=z_scales[:, t, :],
-                in_=grouped_of["z", t][:].rearrange("p b j -> p (b j)"),
-            )
-
         def output_z(t):
             z_ps = ps_bank.tile([P, LATENT], F32, tag="bank")
             for g in range(PASSES_1):
@@ -187,38 +189,62 @@ def tile_ace_pa_kernel(tc, h_enc, enc_w2, enc_b2, clus_w, clus_b, out_0, out_1):
                 op=ALU.add,
             )
 
-        def scores(j, first):
-            split = first >= B_TILES // 2
-            a10 = work.tile([P, GROUP, BANK], F32)
-            a10_of[j, first] = a10
-            for i in range(GROUP):
-                t = first + i
-                bank = ps_bank.tile([P, BANK], F32, tag="bank")
-                nc.tensor.matmul_mx(
-                    out=bank[:],
-                    lhsT=z_codes[:, t, :].bitcast(FP8X4),
-                    lhsT_scale=z_scales[:, t, :],
-                    rhs=w_codes[:, j, :].bitcast(FP8X4),
-                    rhs_scale=w_scales[:, j, :],
-                    start=True,
-                    stop=True,
-                )
-                if split and i == GROUP - 1:
-                    nc.scalar.activation(out=a10[:, i, :], in_=bank[:], func=ACT.Copy, scale=BETA)
-                    nc.gpsimd.tensor_tensor(out=a10[:, i, :], in0=a10[:, i, :], in1=bias10[:, j, :], op=ALU.add)
-                else:
-                    nc.vector.scalar_tensor_tensor(
-                        out=a10[:, i, :], in0=bank[:], scalar=BETA, in1=bias10[:, j, :], op0=ALU.mult, op1=ALU.add
-                    )
+        def quantise_z(t):
+            nc.vector.quantize_mx(
+                out=z_codes[:, t, :].bitcast(FP8X4),
+                scales=z_scales[:, t, :],
+                in_=grouped_of["z", t][:].rearrange("p b j -> p (b j)"),
+            )
 
-        def soft_min(j, first):
-            a10 = a10_of[j, first]
+        def product(n, i):
+            j, t = n // PAIRS, GROUP * (n % PAIRS) + i
+            bank = ps_bank.tile([P, BANK], F32, tag="bank")
+            nc.tensor.matmul_mx(
+                out=bank[:],
+                lhsT=z_codes[:, t, :].bitcast(FP8X4),
+                lhsT_scale=z_scales[:, t, :],
+                rhs=w_codes[:, j, :].bitcast(FP8X4),
+                rhs_scale=w_scales[:, j, :],
+                start=True,
+                stop=True,
+            )
+            return bank
+
+        def is_shared(n):
+            return n in SHARED
+
+        def shared_score(n):
+            a10 = work.tile([P, GROUP, BANK], F32)
+            a10_of[n] = a10
+            if is_shared(n):
+                bank = product(n, 1)
+                nc.scalar.activation(out=a10[:, 1, :], in_=bank[:], func=ACT.Copy, scale=BETA)
+                nc.gpsimd.tensor_tensor(
+                    out=a10[:, 1, :], in0=a10[:, 1, :], in1=bias10[:, n // PAIRS, :], op=ALU.add
+                )
+
+        def scores(n):
+            a10 = a10_of[n]
+            for i in range(GROUP):
+                if i == 1 and is_shared(n):
+                    continue
+                bank = product(n, i)
+                nc.vector.scalar_tensor_tensor(
+                    out=a10[:, i, :], in0=bank[:], scalar=BETA, in1=bias10[:, n // PAIRS, :], op0=ALU.mult, op1=ALU.add
+                )
+
+        def lowest(n):
+            j, first = n // PAIRS, GROUP * (n % PAIRS)
             nc.vector.tensor_reduce(
                 out=low10[:, first : first + GROUP, j * MODS : (j + 1) * MODS],
-                in_=a10[:].rearrange("p i (c k) -> p i c k", k=HEADS),
+                in_=a10_of[n][:].rearrange("p i (c k) -> p i c k", k=HEADS),
                 axis=AXIS.X,
                 op=ALU.min,
             )
+
+        def exps(n):
+            j, first = n // PAIRS, GROUP * (n % PAIRS)
+            a10 = a10_of[n]
             for i in range(GROUP):
                 for c in range(MODS):
                     m = j * MODS + c
@@ -233,58 +259,79 @@ def tile_ace_pa_kernel(tc, h_enc, enc_w2, enc_b2, clus_w, clus_b, out_0, out_1):
 
         with tc.manual_schedule():
             nc.scalar.dma_start(out=b2_pairs[:], in_=enc_b2.bitcast(F32).rearrange("(u q) -> q u", u=2))
-            for g in range(PASSES_1):
-                nc.sync.dma_start(out=w2_raw[:, 2 * g : 2 * g + 2, :], in_=w2_view[:, 2 * g : 2 * g + 2, :])
-            load_h(0)
+            load_w2(0)
+            load_h(0, 2)
+            load_w2(1)
             load_chunk(0)
+            load_h(2, 2)
             load_bias(0)
-            for t in range(2, B_TILES, 2):
-                load_h(t)
-            for j in range(1, CHUNKS):
+            load_h(4, 2)
+            load_chunk(1)
+            load_h(6, 2)
+            for j in range(2, CHUNKS):
                 load_chunk(j)
             for j in range(1, CHUNKS):
                 load_bias(j)
             nc.sync.dma_start(out=b2_free[:], in_=enc_b2.partition_broadcast(P))
             warm_out = keep.tile([P, 1], F32)
             nc.scalar.activation(out=warm_out[:], in_=warm_in[:], func=ACT.Exp)
+            for j in range(CHUNKS):
+                scale_bias(j)
 
-            for g in range(PASSES_1):
-                regroup_w2(g)
-            for g in range(PASSES_1):
-                quantise_w2(g)
+            def both(step, q):
+                for t in range(GROUP * q, GROUP * (q + 1)):
+                    step(t)
+
+            regroup_w2(0)
+            both(flip_h, 0)
+            quantise_w2(0)
+            regroup_w2(1)
+            both(quantise_h, 0)
+            quantise_w2(1)
             nc.vector.tensor_copy(out=b2_part[:], in_=b2_pairs[:].bitcast(BF16))
-            for t in range(GROUP):
-                flip_h(t)
-            flip_chunk(0)
-            for t in range(GROUP):
-                quantise_h(t)
+            flip_chunk(0, 0)
+            flip_chunk(0, 1)
+            both(make_zt, 0)
+            both(flip_h, 1)
+            flip_chunk(1, 0)
+            both(quantise_h, 1)
             quantise_chunk(0)
-
-            groups = [(j, first) for j in range(CHUNKS) for first in range(0, B_TILES, GROUP)]
-            for n, (j, first) in enumerate(groups):
-                if j == 0:
-                    later = range(first + GROUP, min(first + 2 * GROUP, B_TILES))
-                    for t in range(first, first + GROUP):
-                        quantise_z(t)
-                    for t in later:
-                        flip_h(t)
-                    if n > 0:
-                        flip_chunk(n)
-                    for t in later:
-                        quantise_h(t)
-                    for t in range(first, first + GROUP):
-                        quantise_z_codes(t)
-                    if n > 0:
-                        soft_min(*groups[n - 1])
-                scores(j, first)
-                if j > 0 and n < CHUNKS:
-                    flip_chunk(n)
-                if first == GROUP and j + 1 < CHUNKS:
-                    quantise_chunk(j + 1)
-                if j > 0:
-                    soft_min(*groups[n - 1])
-            soft_min(*groups[-1])
-
+            flip_chunk(1, 1)
+            both(quantise_z, 0)
+            for n in range(PAIRS):
+                shared_score(n)
+                scores(n)
+                lowest(n)
+                if n + 2 < PAIRS:
+                    both(flip_h, n + 2)
+                if n + 1 < PAIRS:
+                    both(make_zt, n + 1)
+                if n + 2 < PAIRS:
+                    both(quantise_h, n + 2)
+                if n + 1 < PAIRS:
+                    both(quantise_z, n + 1)
+                exps(n)
+                flip_chunk(n + 2, 0)
+                flip_chunk(n + 2, 1)
+                if n == 1:
+                    quantise_chunk(1)
+            for n in range(PAIRS, CHUNKS * PAIRS):
+                if n == PAIRS:
+                    shared_score(n)
+                scores(n)
+                if n + 1 < CHUNKS * PAIRS:
+                    shared_score(n + 1)
+                if n > PAIRS:
+                    lowest(n - 1)
+                if n + 2 < CHUNKS:
+                    flip_chunk(n + 2, 0)
+                    flip_chunk(n + 2, 1)
+                if n > PAIRS:
+                    exps(n - 1)
+                if n % PAIRS == 1 and n // PAIRS + 1 < CHUNKS:
+                    quantise_chunk(n // PAIRS + 1)
+            lowest(CHUNKS * PAIRS - 1)
+            exps(CHUNKS * PAIRS - 1)
             for t in range(B_TILES):
                 output_z(t)
                 if t % 2 == 1:

@@ -22,7 +22,11 @@ MODS = BANK // HEADS
 ROW_TILES = BANK // P
 GROUP = 2
 PAIRS = B_TILES // GROUP
-SHARED = range(5, 32, 4)
+WIDE = range(1, CHUNKS - 2)
+SUM_LAG = 7
+END_LAG = 1
+FOLD = 8
+SHARED = range(6, 32, 2)
 
 FLOPS = 2 * BATCH * HIDDEN * LATENT + 2 * BATCH * LATENT * MODULES * HEADS
 
@@ -37,8 +41,8 @@ def tile_ace_pa_kernel(tc, h_enc, enc_w2, enc_b2, clus_w, clus_b, out_0, out_1):
     w2_view = enc_w2.rearrange("(w p e) d -> p w (e d)", w=2 * PASSES_1, e=2)
 
     with tc.tile_pool(name="keep", bufs=1) as keep, tc.tile_pool(name="stage", bufs=4) as stage, tc.tile_pool(
-        name="chunks", bufs=8
-    ) as chunks, tc.tile_pool(name="work", bufs=8) as work, tc.psum_pool(name="ps_flip", bufs=4) as ps_flip, tc.psum_pool(name="ps_bank", bufs=4) as ps_bank:
+        name="chunks", bufs=6
+    ) as chunks, tc.tile_pool(name="work", bufs=3) as work, tc.psum_pool(name="ps_flip", bufs=3) as ps_flip, tc.psum_pool(name="ps_bank", bufs=4) as ps_bank, tc.psum_pool(name="ps_sum", bufs=1) as ps_sum:
         ident = keep.tile([P, P], F32)
         make_identity(nc, ident[:])
         warm_in = keep.tile([P, 1], F32)
@@ -67,6 +71,9 @@ def tile_ace_pa_kernel(tc, h_enc, enc_w2, enc_b2, clus_w, clus_b, out_0, out_1):
         low10 = keep.tile([P, B_TILES, MODULES], F32)
         sums = keep.tile([P, B_TILES, MODULES], F32)
         grouped_of = {}
+        parts = ps_sum.tile([P, 2, PAIRS * MODS * FOLD], F32, tag="sum")
+        bank_of = {}
+        chunk_of = {}
         a10_of = {}
 
         def load_h(t, count):
@@ -213,11 +220,19 @@ def tile_ace_pa_kernel(tc, h_enc, enc_w2, enc_b2, clus_w, clus_b, out_0, out_1):
         def is_shared(n):
             return n in SHARED
 
+        def products(n):
+            for i in (1, 0) if is_shared(n) else (0, 1):
+                bank_of[n, i] = product(n, i)
+
         def shared_score(n):
-            a10 = work.tile([P, GROUP, BANK], F32)
+            j, q = n // PAIRS, n % PAIRS
+            if q == 0:
+                a10_tile = work.tile([P, PAIRS, GROUP, BANK], F32)
+                chunk_of[j] = a10_tile
+            a10 = chunk_of[j][:, q, :, :]
             a10_of[n] = a10
             if is_shared(n):
-                bank = product(n, 1)
+                bank = bank_of[n, 1]
                 nc.scalar.activation(out=a10[:, 1, :], in_=bank[:], func=ACT.Copy, scale=BETA)
                 nc.gpsimd.tensor_tensor(
                     out=a10[:, 1, :], in0=a10[:, 1, :], in1=bias10[:, n // PAIRS, :], op=ALU.add
@@ -228,7 +243,7 @@ def tile_ace_pa_kernel(tc, h_enc, enc_w2, enc_b2, clus_w, clus_b, out_0, out_1):
             for i in range(GROUP):
                 if i == 1 and is_shared(n):
                     continue
-                bank = product(n, i)
+                bank = bank_of[n, i]
                 nc.vector.scalar_tensor_tensor(
                     out=a10[:, i, :], in0=bank[:], scalar=BETA, in1=bias10[:, n // PAIRS, :], op0=ALU.mult, op1=ALU.add
                 )
@@ -237,15 +252,58 @@ def tile_ace_pa_kernel(tc, h_enc, enc_w2, enc_b2, clus_w, clus_b, out_0, out_1):
             j, first = n // PAIRS, GROUP * (n % PAIRS)
             nc.vector.tensor_reduce(
                 out=low10[:, first : first + GROUP, j * MODS : (j + 1) * MODS],
-                in_=a10_of[n][:].rearrange("p i (c k) -> p i c k", k=HEADS),
+                in_=a10_of[n].rearrange("p i (c k) -> p i c k", k=HEADS),
                 axis=AXIS.X,
                 op=ALU.min,
             )
+
+        def is_wide(n, i):
+            return i == 0 and n // PAIRS in WIDE
+
+        def centre(n):
+            if is_wide(n, 0):
+                j, t = n // PAIRS, GROUP * (n % PAIRS)
+                a10 = a10_of[n][:, 0, :].rearrange("p (c k) -> p c k", k=HEADS)
+                low = low10[:, t, j * MODS : (j + 1) * MODS].unsqueeze(2).to_broadcast([P, MODS, HEADS])
+                nc.gpsimd.tensor_tensor(out=a10, in0=low, in1=a10, op=ALU.subtract)
+
+        def wide_exp(n):
+            if is_wide(n, 0):
+                nc.scalar.activation(out=a10_of[n][:, 0, :], in_=a10_of[n][:, 0, :], func=ACT.Exp)
+
+        def wide_sum(j, quarter):
+            e = chunk_of[j][:, :, 0, :].rearrange("p q (c k) -> p q c k", k=HEADS)
+            for i in range(2 * quarter, 2 * quarter + 2):
+                nc.tensor.matmul(
+                    parts[:, j % 2, :],
+                    lhsT=ident[:],
+                    rhs=e[:, :, :, i * FOLD : (i + 1) * FOLD],
+                    start=(i == 0),
+                    stop=(i == HEADS // FOLD - 1),
+                )
+
+        def end_sum(j):
+            nc.vector.tensor_reduce(
+                out=sums[:, 0:B_TILES:GROUP, j * MODS : (j + 1) * MODS],
+                in_=parts[:, j % 2, :].rearrange("p (q c r) -> p q c r", q=PAIRS, r=FOLD),
+                axis=AXIS.X,
+                op=ALU.add,
+            )
+
+        def sum_step(n):
+            j, quarter = (n - SUM_LAG) // PAIRS, (n - SUM_LAG) % PAIRS
+            if j in WIDE:
+                wide_sum(j, quarter)
+            j, rest = (n - SUM_LAG - PAIRS - END_LAG) // PAIRS, (n - SUM_LAG - PAIRS - END_LAG) % PAIRS
+            if rest == 0 and j in WIDE:
+                end_sum(j)
 
         def exps(n):
             j, first = n // PAIRS, GROUP * (n % PAIRS)
             a10 = a10_of[n]
             for i in range(GROUP):
+                if is_wide(n, i):
+                    continue
                 for c in range(MODS):
                     m = j * MODS + c
                     nc.scalar.activation(
@@ -262,8 +320,8 @@ def tile_ace_pa_kernel(tc, h_enc, enc_w2, enc_b2, clus_w, clus_b, out_0, out_1):
             load_w2(0)
             load_h(0, 2)
             load_w2(1)
-            load_chunk(0)
             load_h(2, 2)
+            load_chunk(0)
             load_bias(0)
             load_h(4, 2)
             load_chunk(1)
@@ -279,8 +337,9 @@ def tile_ace_pa_kernel(tc, h_enc, enc_w2, enc_b2, clus_w, clus_b, out_0, out_1):
                 scale_bias(j)
 
             def both(step, q):
-                for t in range(GROUP * q, GROUP * (q + 1)):
-                    step(t)
+                if q < PAIRS:
+                    for t in range(GROUP * q, GROUP * (q + 1)):
+                        step(t)
 
             regroup_w2(0)
             both(flip_h, 0)
@@ -289,51 +348,56 @@ def tile_ace_pa_kernel(tc, h_enc, enc_w2, enc_b2, clus_w, clus_b, out_0, out_1):
             both(quantise_h, 0)
             quantise_w2(1)
             nc.vector.tensor_copy(out=b2_part[:], in_=b2_pairs[:].bitcast(BF16))
-            flip_chunk(0, 0)
-            flip_chunk(0, 1)
-            both(make_zt, 0)
             both(flip_h, 1)
-            flip_chunk(1, 0)
+            flip_chunk(0, 0)
             both(quantise_h, 1)
+            both(make_zt, 0)
+            flip_chunk(0, 1)
             quantise_chunk(0)
-            flip_chunk(1, 1)
             both(quantise_z, 0)
+            both(flip_h, 2)
+            both(make_zt, 1)
             for n in range(PAIRS):
+                products(n)
                 shared_score(n)
                 scores(n)
+                flip_chunk(n + 1, 0)
+                flip_chunk(n + 1, 1)
+                both(quantise_h, n + 2)
                 lowest(n)
-                if n + 2 < PAIRS:
-                    both(flip_h, n + 2)
-                if n + 1 < PAIRS:
-                    both(make_zt, n + 1)
-                if n + 2 < PAIRS:
-                    both(quantise_h, n + 2)
-                if n + 1 < PAIRS:
-                    both(quantise_z, n + 1)
+                both(flip_h, n + 3)
+                both(quantise_z, n + 1)
+                both(make_zt, n + 2)
                 exps(n)
-                flip_chunk(n + 2, 0)
-                flip_chunk(n + 2, 1)
                 if n == 1:
                     quantise_chunk(1)
             for n in range(PAIRS, CHUNKS * PAIRS):
                 if n == PAIRS:
+                    products(n)
                     shared_score(n)
                 scores(n)
                 if n + 1 < CHUNKS * PAIRS:
+                    products(n + 1)
                     shared_score(n + 1)
                 if n > PAIRS:
                     lowest(n - 1)
-                if n + 2 < CHUNKS:
-                    flip_chunk(n + 2, 0)
-                    flip_chunk(n + 2, 1)
+                    centre(n - 1)
+                sum_step(n)
+                if n + 1 < CHUNKS:
+                    flip_chunk(n + 1, 0)
+                    flip_chunk(n + 1, 1)
                 if n > PAIRS:
                     exps(n - 1)
+                if n > PAIRS + 1:
+                    wide_exp(n - 2)
                 if n % PAIRS == 1 and n // PAIRS + 1 < CHUNKS:
                     quantise_chunk(n // PAIRS + 1)
-            lowest(CHUNKS * PAIRS - 1)
-            exps(CHUNKS * PAIRS - 1)
+            last = CHUNKS * PAIRS - 1
+            lowest(last)
+            exps(last)
             for t in range(B_TILES):
                 output_z(t)
+                sum_step(last + 1 + t)
                 if t % 2 == 1:
                     nc.sync.dma_start(out=z_view[:, t - 1 : t + 1, :], in_=z_sb[:, t - 1 : t + 1, :])
 

import concourse.mybir as mybir
from concourse.masks import make_identity

F32 = mybir.dt.float32
BF16 = mybir.dt.bfloat16
U32 = mybir.dt.uint32
U8 = mybir.dt.uint8
FP8X4 = mybir.dt.float8_e4m3fn_x4
ALU = mybir.AluOpType
ACT = mybir.ActivationFunctionType
AXIS = mybir.AxisListType

P = 128
PACK = 4
BATCH, HIDDEN, LATENT, MODULES, HEADS = 1024, 1024, 512, 64, 64
BETA = 10.0
B_TILES = BATCH // P
PASSES_1 = HIDDEN // (P * PACK)
BANK = 512
CHUNKS = MODULES * HEADS // BANK
MODS = BANK // HEADS
ROW_TILES = BANK // P
GROUP = 2
PAIRS = B_TILES // GROUP
WIDE = range(1, CHUNKS - 2)
SUM_LAG = 7
END_LAG = 1
FOLD = 8
SHARED = range(6, 32, 2)

FLOPS = 2 * BATCH * HIDDEN * LATENT + 2 * BATCH * LATENT * MODULES * HEADS


def tile_ace_pa_kernel(tc, h_enc, enc_w2, enc_b2, clus_w, clus_b, out_0, out_1):
    nc = tc.nc
    h_view = h_enc.rearrange("(p t) k -> p t k", t=B_TILES)
    z_view = out_0.rearrange("(p t) d -> p t d", t=B_TILES)
    conf_view = out_1.rearrange("(p t) c -> p (t c)", t=B_TILES)
    cw_view = clus_w.rearrange("c k d -> (c k) d").rearrange("(r p) d -> p r d", p=P)
    cb_view = clus_b.rearrange("c k -> (c k)")
    w2_view = enc_w2.rearrange("(w p e) d -> p w (e d)", w=2 * PASSES_1, e=2)

    with tc.tile_pool(name="keep", bufs=1) as keep, tc.tile_pool(name="stage", bufs=4) as stage, tc.tile_pool(
        name="chunks", bufs=6
    ) as chunks, tc.tile_pool(name="work", bufs=3) as work, tc.psum_pool(name="ps_flip", bufs=3) as ps_flip, tc.psum_pool(name="ps_bank", bufs=4) as ps_bank, tc.psum_pool(name="ps_sum", bufs=1) as ps_sum:
        ident = keep.tile([P, P], F32)
        make_identity(nc, ident[:])
        warm_in = keep.tile([P, 1], F32)
        nc.vector.memset(warm_in[:], 1.0)

        w2_raw = keep.tile([P, 2 * PASSES_1, 2 * LATENT], BF16)
        h_sb = keep.tile([P, B_TILES * HIDDEN], BF16)
        cw_sb = keep.tile([P, CHUNKS * ROW_TILES * LATENT], BF16)
        h_words = h_sb[:].bitcast(F32)
        cw_words = cw_sb[:].bitcast(F32)
        cb_free = keep.tile([P, CHUNKS, BANK], BF16)
        bias10 = keep.tile([P, CHUNKS, BANK], F32)
        b2_free = keep.tile([P, LATENT], BF16)
        b2_pairs = keep.tile([P, 2], F32)
        b2_part = keep.tile([P, PACK], F32)
        w2_grouped = keep.tile([P, PASSES_1, LATENT, PACK], BF16, align_bytes=64)
        w2_codes = keep.tile([P, PASSES_1, LATENT], U32, align_bytes=64)
        w2_scales = keep.tile([P, PASSES_1, LATENT], U8, align_bytes=64)
        w_codes = keep.tile([P, CHUNKS, BANK], U32, align_bytes=64)
        w_scales = keep.tile([P, CHUNKS, BANK], U8, align_bytes=64)
        h_codes = keep.tile([P, B_TILES, PASSES_1 * P], U32, align_bytes=64)
        h_scales = keep.tile([P, B_TILES, PASSES_1 * P], U8, align_bytes=64)
        z_sb = keep.tile([P, B_TILES, LATENT], F32)
        z_codes = keep.tile([P, B_TILES, P], U32, align_bytes=64)
        z_scales = keep.tile([P, B_TILES, P], U8, align_bytes=64)
        low10 = keep.tile([P, B_TILES, MODULES], F32)
        sums = keep.tile([P, B_TILES, MODULES], F32)
        grouped_of = {}
        parts = ps_sum.tile([P, 2, PAIRS * MODS * FOLD], F32, tag="sum")
        bank_of = {}
        chunk_of = {}
        a10_of = {}

        def load_h(t, count):
            nc.sync.dma_start(
                out=h_sb[:, t * HIDDEN : (t + count) * HIDDEN].rearrange("p (t k) -> p t k", t=count),
                in_=h_view[:, t : t + count, :],
            )

        def load_w2(g):
            nc.sync.dma_start(out=w2_raw[:, 2 * g : 2 * g + 2, :], in_=w2_view[:, 2 * g : 2 * g + 2, :])

        def load_chunk(j):
            nc.sync.dma_start(
                out=cw_sb[:, j * ROW_TILES * LATENT : (j + 1) * ROW_TILES * LATENT].rearrange(
                    "p (r d) -> p r d", r=ROW_TILES
                ),
                in_=cw_view[:, j * ROW_TILES : (j + 1) * ROW_TILES, :],
            )

        def load_bias(j):
            nc.sync.dma_start(out=cb_free[:, j, :], in_=cb_view[j * BANK : (j + 1) * BANK].partition_broadcast(P))

        def scale_bias(j):
            nc.gpsimd.tensor_scalar(
                out=bias10[:, j, :], in0=cb_free[:, j, :], scalar1=BETA, scalar2=0.0, op0=ALU.mult, op1=ALU.add
            )

        def regroup_w2(g):
            for u in range(2):
                nc.vector.tensor_copy(
                    out=w2_grouped[:, g, 256 * u : 256 * (u + 1), :].rearrange("p (e q) j -> p e q j", e=2),
                    in_=w2_raw[:, 2 * g : 2 * g + 2, :]
                    .rearrange("p w (e d) -> p (w e) d", e=2)[:, :, 256 * u : 256 * (u + 1)]
                    .rearrange("p j (q e) -> p e q j", e=2),
                )

        def quantise_w2(g):
            nc.vector.quantize_mx(
                out=w2_codes[:, g, :].bitcast(FP8X4),
                scales=w2_scales[:, g, :],
                in_=w2_grouped[:, g, :, :].rearrange("p d j -> p (d j)"),
            )

        def flip_chunk(j, half):
            if half == 0:
                w_tile = chunks.tile([P, BANK * PACK], BF16, align_bytes=64)
                grouped_of["w", j] = w_tile
            w_grouped = grouped_of["w", j]
            flip_w = ps_flip.tile([P, PACK, P], F32, tag="flip")
            for u in range(2):
                for rr in range(2):
                    r = j * ROW_TILES + 2 * half + rr
                    nc.tensor.transpose(
                        flip_w[:, 2 * u + rr, :], cw_words[:, r * 256 + u * P : r * 256 + (u + 1) * P], ident[:]
                    )
            nc.scalar.copy(
                out=w_grouped[:, half * 1024 : (half + 1) * 1024].bitcast(F32).rearrange("p (n u) -> p n u", u=2),
                in_=flip_w[:].rearrange("p (u r) q -> p (r q) u", u=2),
            )

        def quantise_chunk(j):
            nc.vector.quantize_mx(
                out=w_codes[:, j, :].bitcast(FP8X4), scales=w_scales[:, j, :], in_=grouped_of["w", j][:]
            )

        def flip_h(t):
            flip = ps_flip.tile([P, PACK, P], F32, tag="flip")
            for w in range(2 * PASSES_1):
                nc.tensor.transpose(flip[:, w, :], h_words[:, t * 512 + w * P : t * 512 + (w + 1) * P], ident[:])
            h_grouped = stage.tile([P, PASSES_1 * P * PACK], BF16, align_bytes=64)
            grouped_of["h", t] = h_grouped
            nc.scalar.copy(
                out=h_grouped[:].bitcast(F32).rearrange("p (g b u) -> p g b u", g=PASSES_1, u=2),
                in_=flip[:].rearrange("p (g u) b -> p g b u", u=2),
            )

        def quantise_h(t):
            nc.vector.quantize_mx(
                out=h_codes[:, t, :].bitcast(FP8X4), scales=h_scales[:, t, :], in_=grouped_of["h", t][:]
            )

        def make_zt(t):
            zt_ps = ps_bank.tile([P, PACK, P], F32, tag="bank")
            for j in range(PACK):
                for g in range(PASSES_1):
                    nc.tensor.matmul_mx(
                        out=zt_ps[:, j, :],
                        lhsT=w2_codes[:, g, j * P : (j + 1) * P].bitcast(FP8X4),
                        lhsT_scale=w2_scales[:, g, j * P : (j + 1) * P],
                        rhs=h_codes[:, t, g * P : (g + 1) * P].bitcast(FP8X4),
                        rhs_scale=h_scales[:, t, g * P : (g + 1) * P],
                        start=(g == 0),
                        stop=(g == PASSES_1 - 1),
                    )
            z_grouped = stage.tile([P, P, PACK], BF16, align_bytes=64)
            grouped_of["z", t] = z_grouped
            nc.vector.tensor_tensor(
                out=z_grouped[:],
                in0=zt_ps[:].rearrange("p j b -> p b j"),
                in1=b2_part[:].unsqueeze(1).to_broadcast([P, P, PACK]),
                op=ALU.add,
            )

        def output_z(t):
            z_ps = ps_bank.tile([P, LATENT], F32, tag="bank")
            for g in range(PASSES_1):
                nc.tensor.matmul_mx(
                    out=z_ps[:],
                    lhsT=h_codes[:, t, g * P : (g + 1) * P].bitcast(FP8X4),
                    lhsT_scale=h_scales[:, t, g * P : (g + 1) * P],
                    rhs=w2_codes[:, g, :].bitcast(FP8X4),
                    rhs_scale=w2_scales[:, g, :],
                    start=(g == 0),
                    stop=(g == PASSES_1 - 1),
                )
            nc.vector.tensor_tensor(
                out=z_sb[:, t, :].rearrange("p (u q e) -> p u q e", u=2, e=2),
                in0=z_ps[:].rearrange("p (u e q) -> p u q e", u=2, e=2),
                in1=b2_free[:].rearrange("p (u q e) -> p u q e", u=2, e=2),
                op=ALU.add,
            )

        def quantise_z(t):
            nc.vector.quantize_mx(
                out=z_codes[:, t, :].bitcast(FP8X4),
                scales=z_scales[:, t, :],
                in_=grouped_of["z", t][:].rearrange("p b j -> p (b j)"),
            )

        def product(n, i):
            j, t = n // PAIRS, GROUP * (n % PAIRS) + i
            bank = ps_bank.tile([P, BANK], F32, tag="bank")
            nc.tensor.matmul_mx(
                out=bank[:],
                lhsT=z_codes[:, t, :].bitcast(FP8X4),
                lhsT_scale=z_scales[:, t, :],
                rhs=w_codes[:, j, :].bitcast(FP8X4),
                rhs_scale=w_scales[:, j, :],
                start=True,
                stop=True,
            )
            return bank

        def is_shared(n):
            return n in SHARED

        def products(n):
            for i in (1, 0) if is_shared(n) else (0, 1):
                bank_of[n, i] = product(n, i)

        def shared_score(n):
            j, q = n // PAIRS, n % PAIRS
            if q == 0:
                a10_tile = work.tile([P, PAIRS, GROUP, BANK], F32)
                chunk_of[j] = a10_tile
            a10 = chunk_of[j][:, q, :, :]
            a10_of[n] = a10
            if is_shared(n):
                bank = bank_of[n, 1]
                nc.scalar.activation(out=a10[:, 1, :], in_=bank[:], func=ACT.Copy, scale=BETA)
                nc.gpsimd.tensor_tensor(
                    out=a10[:, 1, :], in0=a10[:, 1, :], in1=bias10[:, n // PAIRS, :], op=ALU.add
                )

        def scores(n):
            a10 = a10_of[n]
            for i in range(GROUP):
                if i == 1 and is_shared(n):
                    continue
                bank = bank_of[n, i]
                nc.vector.scalar_tensor_tensor(
                    out=a10[:, i, :], in0=bank[:], scalar=BETA, in1=bias10[:, n // PAIRS, :], op0=ALU.mult, op1=ALU.add
                )

        def lowest(n):
            j, first = n // PAIRS, GROUP * (n % PAIRS)
            nc.vector.tensor_reduce(
                out=low10[:, first : first + GROUP, j * MODS : (j + 1) * MODS],
                in_=a10_of[n].rearrange("p i (c k) -> p i c k", k=HEADS),
                axis=AXIS.X,
                op=ALU.min,
            )

        def is_wide(n, i):
            return i == 0 and n // PAIRS in WIDE

        def centre(n):
            if is_wide(n, 0):
                j, t = n // PAIRS, GROUP * (n % PAIRS)
                a10 = a10_of[n][:, 0, :].rearrange("p (c k) -> p c k", k=HEADS)
                low = low10[:, t, j * MODS : (j + 1) * MODS].unsqueeze(2).to_broadcast([P, MODS, HEADS])
                nc.gpsimd.tensor_tensor(out=a10, in0=low, in1=a10, op=ALU.subtract)

        def wide_exp(n):
            if is_wide(n, 0):
                nc.scalar.activation(out=a10_of[n][:, 0, :], in_=a10_of[n][:, 0, :], func=ACT.Exp)

        def wide_sum(j, quarter):
            e = chunk_of[j][:, :, 0, :].rearrange("p q (c k) -> p q c k", k=HEADS)
            for i in range(2 * quarter, 2 * quarter + 2):
                nc.tensor.matmul(
                    parts[:, j % 2, :],
                    lhsT=ident[:],
                    rhs=e[:, :, :, i * FOLD : (i + 1) * FOLD],
                    start=(i == 0),
                    stop=(i == HEADS // FOLD - 1),
                )

        def end_sum(j):
            nc.vector.tensor_reduce(
                out=sums[:, 0:B_TILES:GROUP, j * MODS : (j + 1) * MODS],
                in_=parts[:, j % 2, :].rearrange("p (q c r) -> p q c r", q=PAIRS, r=FOLD),
                axis=AXIS.X,
                op=ALU.add,
            )

        def sum_step(n):
            j, quarter = (n - SUM_LAG) // PAIRS, (n - SUM_LAG) % PAIRS
            if j in WIDE:
                wide_sum(j, quarter)
            j, rest = (n - SUM_LAG - PAIRS - END_LAG) // PAIRS, (n - SUM_LAG - PAIRS - END_LAG) % PAIRS
            if rest == 0 and j in WIDE:
                end_sum(j)

        def exps(n):
            j, first = n // PAIRS, GROUP * (n % PAIRS)
            a10 = a10_of[n]
            for i in range(GROUP):
                if is_wide(n, i):
                    continue
                for c in range(MODS):
                    m = j * MODS + c
                    nc.scalar.activation(
                        out=a10[:, i, c * HEADS : (c + 1) * HEADS],
                        in_=a10[:, i, c * HEADS : (c + 1) * HEADS],
                        func=ACT.Exp,
                        bias=low10[:, first + i, m : m + 1],
                        scale=-1.0,
                        accum_out=sums[:, first + i, m : m + 1],
                    )

        with tc.manual_schedule():
            nc.scalar.dma_start(out=b2_pairs[:], in_=enc_b2.bitcast(F32).rearrange("(u q) -> q u", u=2))
            load_w2(0)
            load_h(0, 2)
            load_w2(1)
            load_h(2, 2)
            load_chunk(0)
            load_bias(0)
            load_h(4, 2)
            load_chunk(1)
            load_h(6, 2)
            for j in range(2, CHUNKS):
                load_chunk(j)
            for j in range(1, CHUNKS):
                load_bias(j)
            nc.sync.dma_start(out=b2_free[:], in_=enc_b2.partition_broadcast(P))
            warm_out = keep.tile([P, 1], F32)
            nc.scalar.activation(out=warm_out[:], in_=warm_in[:], func=ACT.Exp)
            for j in range(CHUNKS):
                scale_bias(j)

            def both(step, q):
                if q < PAIRS:
                    for t in range(GROUP * q, GROUP * (q + 1)):
                        step(t)

            regroup_w2(0)
            both(flip_h, 0)
            quantise_w2(0)
            regroup_w2(1)
            both(quantise_h, 0)
            quantise_w2(1)
            nc.vector.tensor_copy(out=b2_part[:], in_=b2_pairs[:].bitcast(BF16))
            both(flip_h, 1)
            flip_chunk(0, 0)
            both(quantise_h, 1)
            both(make_zt, 0)
            flip_chunk(0, 1)
            quantise_chunk(0)
            both(quantise_z, 0)
            both(flip_h, 2)
            both(make_zt, 1)
            for n in range(PAIRS):
                products(n)
                shared_score(n)
                scores(n)
                flip_chunk(n + 1, 0)
                flip_chunk(n + 1, 1)
                both(quantise_h, n + 2)
                lowest(n)
                both(flip_h, n + 3)
                both(quantise_z, n + 1)
                both(make_zt, n + 2)
                exps(n)
                if n == 1:
                    quantise_chunk(1)
            for n in range(PAIRS, CHUNKS * PAIRS):
                if n == PAIRS:
                    products(n)
                    shared_score(n)
                scores(n)
                if n + 1 < CHUNKS * PAIRS:
                    products(n + 1)
                    shared_score(n + 1)
                if n > PAIRS:
                    lowest(n - 1)
                    centre(n - 1)
                sum_step(n)
                if n + 1 < CHUNKS:
                    flip_chunk(n + 1, 0)
                    flip_chunk(n + 1, 1)
                if n > PAIRS:
                    exps(n - 1)
                if n > PAIRS + 1:
                    wide_exp(n - 2)
                if n % PAIRS == 1 and n // PAIRS + 1 < CHUNKS:
                    quantise_chunk(n // PAIRS + 1)
            last = CHUNKS * PAIRS - 1
            lowest(last)
            exps(last)
            for t in range(B_TILES):
                output_z(t)
                sum_step(last + 1 + t)
                if t % 2 == 1:
                    nc.sync.dma_start(out=z_view[:, t - 1 : t + 1, :], in_=z_sb[:, t - 1 : t + 1, :])

            log_sums = keep.tile([P, B_TILES * MODULES], F32)
            nc.scalar.activation(out=log_sums[:], in_=sums[:].rearrange("p t c -> p (t c)"), func=ACT.Ln)
            conf = keep.tile([P, B_TILES * MODULES], F32)
            nc.vector.tensor_tensor(
                out=conf[:], in0=low10[:].rearrange("p t c -> p (t c)"), in1=log_sums[:], op=ALU.subtract
            )
            nc.sync.dma_start(out=conf_view, in_=conf[:])
